import numpy as np
import ml_dtypes


def mxq(x, axis, fmt="e4m3"):
    dtype, down = {"e4m3": (ml_dtypes.float8_e4m3fn, 7), "e5m2": (ml_dtypes.float8_e5m2, 14)}[fmt]
    v = np.moveaxis(np.asarray(x, np.float32).astype(ml_dtypes.bfloat16).astype(np.float64), axis, -1)
    blocks = v.reshape(v.shape[:-1] + (-1, 32))
    amax = np.abs(blocks).max(-1, keepdims=True)
    byte = np.maximum(np.where(amax > 0, np.frexp(amax)[1] - 1 + 127, 0) - down, 1)
    scale = np.exp2(byte - 127.0)
    codes = (blocks / scale).astype(np.float32).astype(dtype).astype(np.float64)
    return np.moveaxis((codes * scale).reshape(v.shape), -1, axis)


WIDE = False


def mx_kscale(k):
    if not WIDE:
        return np.ones(k)
    levels = np.array([10, -10, 5, -5, 0])
    if k % 512:
        return np.exp2(np.random.permutation(np.resize(levels, k // 32))).repeat(32)
    a = np.empty((k // 512, 16))
    for p in range(k // 512):
        a[p, :8] = np.random.permutation(np.resize(levels, 8))
        for g in range(8):
            far = levels[np.abs(levels - a[p, g]) >= 10]
            a[p, g + 8] = far[np.random.randint(len(far))]
    return np.exp2(a.ravel()).repeat(32)


BF16 = ml_dtypes.bfloat16


def bf(x):
    return np.asarray(x, np.float32).astype(BF16)


def f64(x):
    return np.asarray(x).astype(np.float64)


B, S, I0, I1, I2, N0, N1, N2 = 4, 256, 512, 1024, 2048, 512, 512, 1024


def blk(fan_in, width, s):
    return bf(np.random.uniform(-1.0, 1.0, (fan_in, width)) / np.sqrt(fan_in) / s[:fan_in, None])


def setup_inputs():
    s = mx_kscale(I2)
    return {"x": bf(np.random.standard_normal((B, S, I2)) * s),
            "w0": blk(I0, N0, s), "w1": blk(I1, N1, s), "w2": blk(I2, N2, s),
            "bias": bf(np.random.standard_normal(N0 + N1 + N2) * 0.1)}


def reference(x, w0, w1, w2, bias):
    xq = mxq(f64(x), 2, "e4m3")
    y0 = xq[:, :, :I0] @ mxq(f64(w0), 0, "e4m3")
    y1 = xq[:, :, :I1] @ mxq(f64(w1), 0, "e4m3")
    y2 = xq @ mxq(f64(w2), 0, "e4m3")
    return np.concatenate([y0, y1, y2], axis=2) + f64(bias)

@@ -1,0 +1,201 @@
+from contextlib import ExitStack
+
+import concourse.mybir as mybir
+from concourse.masks import make_identity
+
+F32 = mybir.dt.float32
+BF16 = mybir.dt.bfloat16
+U32 = mybir.dt.uint32
+U8 = mybir.dt.uint8
+I32 = mybir.dt.int32
+FP8X4 = mybir.dt.float8_e4m3fn_x4
+ADD = mybir.AluOpType.add
+
+P = 128
+TILES = 8
+FEAT = 2048
+NOUT = 2048
+NB = 512
+FLOPS = 2 * 1024 * (512 * 512 + 1024 * 512 + 2048 * 1024)
+
+PINNED = False
+CHUNKS = [(0, 0)] + [(1, g) for g in range(2)] + [(2, g) for g in range(4)] + [(3, g) for g in range(4)]
+PASSES = [1, 2, 4, 4]
+VSHARE = [4, 2, 1, 2, 1, 0, 0, 1, 0, 0, 0]
+
+
+def tile_mlinear_kernel(tc, x, w0, w1, w2, bias, out):
+    nc = tc.nc
+    xv = x.flatten_outer_dims().rearrange("(p i) f -> p i f", i=TILES)
+    ov = out.flatten_outer_dims().rearrange("(p i) n -> p i n", i=TILES)
+
+    with ExitStack() as ctx:
+        if PINNED:
+            ctx.enter_context(tc.manual_schedule())
+        const = ctx.enter_context(tc.tile_pool(name="const", bufs=1))
+        xin = ctx.enter_context(tc.tile_pool(name="xin", bufs=1))
+        xgp = ctx.enter_context(tc.tile_pool(name="xgp", bufs=3))
+        xq = ctx.enter_context(tc.tile_pool(name="xq", bufs=1))
+        win = ctx.enter_context(tc.tile_pool(name="win", bufs=1))
+        wgp = ctx.enter_context(tc.tile_pool(name="wgp", bufs=4))
+        wq = ctx.enter_context(tc.tile_pool(name="wq", bufs=1))
+        outp = ctx.enter_context(tc.tile_pool(name="outp", bufs=1))
+        ps = ctx.enter_context(tc.psum_pool(name="ps", bufs=1))
+
+        zb = const.tile([P, NOUT], BF16, name="zb")
+        ones = const.tile([P, P], BF16, name="ones")
+        ident = const.tile([P, P], F32, name="ident")
+        bias_bc = const.tile([P, NOUT], BF16, name="bias_bc")
+        nc.vector.memset(zb[:].bitcast(I32), 0)
+        nc.vector.memset(ones[:], 1.0)
+        make_identity(nc, ident[:])
+        nc.sync.dma_start(out=zb[0:1, :], in_=bias.rearrange("(o n) -> o n", o=1))
+
+        x_sb = [xin.tile([P, FEAT], BF16, name="x%d" % i) for i in range(TILES)]
+        w_raw = {}
+        w_raw[(0, 0)] = win.tile([P, 4, NB], BF16, name="w0r")
+        for g in range(2):
+            w_raw[(1, g)] = win.tile([P, 4, NB], BF16, name="w1r%d" % g)
+        for g in range(4):
+            w_raw[(2, g)] = win.tile([P, 4, 2 * NB], BF16, name="w2r%d" % g)
+
+        def load_x(i):
+            nc.sync.dma_start(out=x_sb[i][:], in_=xv[:, i, :])
+
+        def load_w(key, src, g):
+            nc.sync.dma_start(
+                out=w_raw[key][:].rearrange("p t c -> p (t c)"),
+                in_=src[512 * g : 512 * (g + 1), :].rearrange("(p t) c -> p (t c)", p=P, t=4),
+            )
+
+        load_x(0)
+        load_w((0, 0), w0, 0)
+        for i in range(1, TILES):
+            load_x(i)
+        for g in range(2):
+            load_w((1, g), w1, g)
+        for g in range(4):
+            load_w((2, g), w2, g)
+
+        xc = [xq.tile([P, 512], U32, name="xc%d" % i, align_bytes=64) for i in range(TILES)]
+        xs = [xq.tile([P, 512], U8, name="xs%d" % i, align_bytes=64) for i in range(TILES)]
+        wc = [wq.tile([P, NB], U32, name="wc%d" % c, align_bytes=64) for c in range(len(CHUNKS))]
+        ws = [wq.tile([P, NB], U8, name="ws%d" % c, align_bytes=64) for c in range(len(CHUNKS))]
+        o_sb = [outp.tile([P, NOUT], F32, name="o%d" % i) for i in range(TILES)]
+
+        xt = {}
+        xg = {}
+        wg = {}
+        acc = {}
+
+        def transposes(i):
+            xw = x_sb[i][:].bitcast(F32)
+            for h in range(2):
+                t = ps.tile([P, 4, P], F32, name="xt%d_%d" % (i, h), tag="bank%d" % ((2 * i + h) % 4))
+                xt[(i, h)] = t
+                for j in range(4):
+                    b = 4 * h + j
+                    nc.tensor.transpose(t[:, j, :], xw[:, 256 * (b // 2) + b % 2 : 256 * (b // 2 + 1) : 2], ident[:])
+
+        def copies(i):
+            g_t = xgp.tile([P, FEAT], BF16, name="xg%d" % i, tag="xg", align_bytes=64)
+            xg[i] = g_t
+            gw = g_t[:].bitcast(F32)
+            for h in range(2):
+                nc.scalar.copy(
+                    out=gw[:, 512 * h : 512 * (h + 1)].rearrange("p (g r u) -> p g r u", g=2, r=P, u=2),
+                    in_=xt[(i, h)][:].rearrange("p (g u) r -> p g r u", g=2, u=2),
+                )
+
+        def quant_x(i):
+            nc.vector.quantize_mx(out=xc[i][:].bitcast(FP8X4), scales=xs[i][:], in_=xg[i][:])
+
+        def bias_bcast():
+            for h in range(2):
+                pb = ps.tile([P, 1024], BF16, name="pb%d" % h, tag="bank%d" % (6 + h))
+                for j in range(2):
+                    c0 = 1024 * h + 512 * j
+                    nc.tensor.matmul(out=pb[:, 512 * j : 512 * (j + 1)], lhsT=ones[:], rhs=zb[:, c0 : c0 + 512], start=True, stop=True)
+                nc.scalar.copy(out=bias_bc[:, 1024 * h : 1024 * (h + 1)], in_=pb[:])
+
+        def regroup(c):
+            blk, g = CHUNKS[c]
+            if blk < 2:
+                src = w_raw[(blk, g)][:]
+            else:
+                src = w_raw[(2, g)][:, :, NB * (blk - 2) : NB * (blk - 1)]
+            t = wgp.tile([P, NB, 4], BF16, name="wg%d" % c, tag="wg", align_bytes=64)
+            wg[c] = t
+            cut = NB - P * VSHARE[c]
+            if cut > 0:
+                nc.scalar.copy(
+                    out=t[:, 0:cut, :].rearrange("p (c i) t -> p c t i", i=4),
+                    in_=src[:, :, 0:cut].rearrange("p t (c i) -> p c t i", i=4),
+                )
+            if cut < NB:
+                nc.vector.tensor_copy(
+                    out=t[:, cut:NB, :].rearrange("p (c i) t -> p c t i", i=4),
+                    in_=src[:, :, cut:NB].rearrange("p t (c i) -> p c t i", i=4),
+                )
+
+        def quant_w(c):
+            nc.vector.quantize_mx(
+                out=wc[c][:].bitcast(FP8X4), scales=ws[c][:], in_=wg[c][:].rearrange("p c t -> p (c t)")
+            )
+
+        def mx_pass(c, i):
+            blk, g = CHUNKS[c]
+            if g == 0:
+                bank = 4 + i % 4 if blk == 0 else i
+                acc[(blk, i)] = ps.tile([P, NB], F32, name="acc%d_%d" % (blk, i), tag="bank%d" % bank)
+            nc.tensor.matmul_mx(
+                out=acc[(blk, i)][:],
+                lhsT=xc[i][:, P * g : P * (g + 1)].bitcast(FP8X4),
+                lhsT_scale=xs[i][:, P * g : P * (g + 1)],
+                rhs=wc[c][:].bitcast(FP8X4),
+                rhs_scale=ws[c][:],
+                start=(g == 0),
+                stop=(g == PASSES[blk] - 1),
+            )
+
+        def evac(blk, i):
+            cols = slice(NB * blk, NB * (blk + 1))
+            nc.vector.tensor_tensor(out=o_sb[i][:, cols], in0=acc[(blk, i)][:], in1=bias_bc[:, cols], op=ADD)
+
+        def store(i, c0, c1):
+            nc.sync.dma_start(out=ov[:, i, c0:c1], in_=o_sb[i][:, c0:c1])
+
+        transposes(0)
+        copies(0)
+        bias_bcast()
+        regroup(0)
+        quant_x(0)
+        quant_w(0)
+        mx_pass(0, 0)
+        evac(0, 0)
+        for i in range(1, TILES):
+            transposes(i)
+            copies(i)
+            quant_x(i)
+            mx_pass(0, i)
+            evac(0, i)
+        for c in range(1, len(CHUNKS)):
+            regroup(c)
+            quant_w(c)
+        for c in (1, 2):
+            for i in range(TILES):
+                mx_pass(c, i)
+                if c == 2:
+                    evac(1, i)
+                    store(i, 0, 2 * NB)
+        for c in (3, 4, 5, 6):
+            for i in range(TILES):
+                mx_pass(c, i)
+                if c == 6:
+                    evac(2, i)
+                    store(i, 2 * NB, 3 * NB)
+        for i in range(TILES):
+            for c in (7, 8, 9, 10):
+                mx_pass(c, i)
+            evac(3, i)
+            store(i, 3 * NB, 4 * NB)

@@ -93,6 +93,10 @@ def tile_mlinear_kernel(tc, x, w0, w1, w2, bias, out):
             for h in range(2):
                 t = ps.tile([P, 4, P], F32, name="xt%d_%d" % (i, h), tag="bank%d" % ((2 * i + h) % 4))
                 xt[(i, h)] = t
+                if h == 0:
+                    nc.tensor.matmul(
+                        out=t[:].rearrange("p j r -> p (j r)"), lhsT=ones[:], rhs=x_sb[i][:, 0:NB], start=True, stop=True
+                    )
                 for j in range(4):
                     b = 4 * h + j
                     nc.tensor.transpose(t[:, j, :], xw[:, 256 * (b // 2) + b % 2 : 256 * (b // 2 + 1) : 2], ident[:])

@@ -198,8 +198,25 @@ def tile_mlinear_kernel(tc, x, w0, w1, w2, bias, out):
                 if c == 6:
                     evac(2, i)
                     store(i, 2 * NB, 3 * NB)
-        for i in range(TILES):
+        for i in range(TILES - 1):
             for c in (7, 8, 9, 10):
                 mx_pass(c, i)
             evac(3, i)
             store(i, 3 * NB, 4 * NB)
+        last = TILES - 1
+        for h in range(2):
+            half = ps.tile([P, NB // 2], F32, name="half%d" % h, tag="bank%d" % (last if h == 0 else 3))
+            cols = slice(NB // 2 * h, NB // 2 * (h + 1))
+            for g in range(4):
+                nc.tensor.matmul_mx(
+                    out=half[:],
+                    lhsT=xc[last][:, P * g : P * (g + 1)].bitcast(FP8X4),
+                    lhsT_scale=xs[last][:, P * g : P * (g + 1)],
+                    rhs=wc[7 + g][:, cols].bitcast(FP8X4),
+                    rhs_scale=ws[7 + g][:, cols],
+                    start=(g == 0),
+                    stop=(g == 3),
+                )
+            oc = slice(3 * NB + NB // 2 * h, 3 * NB + NB // 2 * (h + 1))
+            nc.vector.tensor_tensor(out=o_sb[last][:, oc], in0=half[:], in1=bias_bc[:, oc], op=ADD)
+            store(last, 3 * NB + NB // 2 * h, 3 * NB + NB // 2 * (h + 1))

from contextlib import ExitStack

import concourse.mybir as mybir
from concourse.masks import make_identity

F32 = mybir.dt.float32
BF16 = mybir.dt.bfloat16
U32 = mybir.dt.uint32
U8 = mybir.dt.uint8
I32 = mybir.dt.int32
FP8X4 = mybir.dt.float8_e4m3fn_x4
ADD = mybir.AluOpType.add

P = 128
TILES = 8
FEAT = 2048
NOUT = 2048
NB = 512
FLOPS = 2 * 1024 * (512 * 512 + 1024 * 512 + 2048 * 1024)

PINNED = False
CHUNKS = [(0, 0)] + [(1, g) for g in range(2)] + [(2, g) for g in range(4)] + [(3, g) for g in range(4)]
PASSES = [1, 2, 4, 4]
VSHARE = [4, 2, 1, 2, 1, 0, 0, 1, 0, 0, 0]


def tile_mlinear_kernel(tc, x, w0, w1, w2, bias, out):
    nc = tc.nc
    xv = x.flatten_outer_dims().rearrange("(p i) f -> p i f", i=TILES)
    ov = out.flatten_outer_dims().rearrange("(p i) n -> p i n", i=TILES)

    with ExitStack() as ctx:
        if PINNED:
            ctx.enter_context(tc.manual_schedule())
        const = ctx.enter_context(tc.tile_pool(name="const", bufs=1))
        xin = ctx.enter_context(tc.tile_pool(name="xin", bufs=1))
        xgp = ctx.enter_context(tc.tile_pool(name="xgp", bufs=3))
        xq = ctx.enter_context(tc.tile_pool(name="xq", bufs=1))
        win = ctx.enter_context(tc.tile_pool(name="win", bufs=1))
        wgp = ctx.enter_context(tc.tile_pool(name="wgp", bufs=4))
        wq = ctx.enter_context(tc.tile_pool(name="wq", bufs=1))
        outp = ctx.enter_context(tc.tile_pool(name="outp", bufs=1))
        ps = ctx.enter_context(tc.psum_pool(name="ps", bufs=1))

        zb = const.tile([P, NOUT], BF16, name="zb")
        ones = const.tile([P, P], BF16, name="ones")
        ident = const.tile([P, P], F32, name="ident")
        bias_bc = const.tile([P, NOUT], BF16, name="bias_bc")
        nc.vector.memset(zb[:].bitcast(I32), 0)
        nc.vector.memset(ones[:], 1.0)
        make_identity(nc, ident[:])
        nc.sync.dma_start(out=zb[0:1, :], in_=bias.rearrange("(o n) -> o n", o=1))

        x_sb = [xin.tile([P, FEAT], BF16, name="x%d" % i) for i in range(TILES)]
        w_raw = {}
        w_raw[(0, 0)] = win.tile([P, 4, NB], BF16, name="w0r")
        for g in range(2):
            w_raw[(1, g)] = win.tile([P, 4, NB], BF16, name="w1r%d" % g)
        for g in range(4):
            w_raw[(2, g)] = win.tile([P, 4, 2 * NB], BF16, name="w2r%d" % g)

        def load_x(i):
            nc.sync.dma_start(out=x_sb[i][:], in_=xv[:, i, :])

        def load_w(key, src, g):
            nc.sync.dma_start(
                out=w_raw[key][:].rearrange("p t c -> p (t c)"),
                in_=src[512 * g : 512 * (g + 1), :].rearrange("(p t) c -> p (t c)", p=P, t=4),
            )

        load_x(0)
        load_w((0, 0), w0, 0)
        for i in range(1, TILES):
            load_x(i)
        for g in range(2):
            load_w((1, g), w1, g)
        for g in range(4):
            load_w((2, g), w2, g)

        xc = [xq.tile([P, 512], U32, name="xc%d" % i, align_bytes=64) for i in range(TILES)]
        xs = [xq.tile([P, 512], U8, name="xs%d" % i, align_bytes=64) for i in range(TILES)]
        wc = [wq.tile([P, NB], U32, name="wc%d" % c, align_bytes=64) for c in range(len(CHUNKS))]
        ws = [wq.tile([P, NB], U8, name="ws%d" % c, align_bytes=64) for c in range(len(CHUNKS))]
        o_sb = [outp.tile([P, NOUT], F32, name="o%d" % i) for i in range(TILES)]

        xt = {}
        xg = {}
        wg = {}
        acc = {}

        def transposes(i):
            xw = x_sb[i][:].bitcast(F32)
            for h in range(2):
                t = ps.tile([P, 4, P], F32, name="xt%d_%d" % (i, h), tag="bank%d" % ((2 * i + h) % 4))
                xt[(i, h)] = t
                if h == 0:
                    nc.tensor.matmul(
                        out=t[:].rearrange("p j r -> p (j r)"), lhsT=ones[:], rhs=x_sb[i][:, 0:NB], start=True, stop=True
                    )
                for j in range(4):
                    b = 4 * h + j
                    nc.tensor.transpose(t[:, j, :], xw[:, 256 * (b // 2) + b % 2 : 256 * (b // 2 + 1) : 2], ident[:])

        def copies(i):
            g_t = xgp.tile([P, FEAT], BF16, name="xg%d" % i, tag="xg", align_bytes=64)
            xg[i] = g_t
            gw = g_t[:].bitcast(F32)
            for h in range(2):
                nc.scalar.copy(
                    out=gw[:, 512 * h : 512 * (h + 1)].rearrange("p (g r u) -> p g r u", g=2, r=P, u=2),
                    in_=xt[(i, h)][:].rearrange("p (g u) r -> p g r u", g=2, u=2),
                )

        def quant_x(i):
            nc.vector.quantize_mx(out=xc[i][:].bitcast(FP8X4), scales=xs[i][:], in_=xg[i][:])

        def bias_bcast():
            for h in range(2):
                pb = ps.tile([P, 1024], BF16, name="pb%d" % h, tag="bank%d" % (6 + h))
                for j in range(2):
                    c0 = 1024 * h + 512 * j
                    nc.tensor.matmul(out=pb[:, 512 * j : 512 * (j + 1)], lhsT=ones[:], rhs=zb[:, c0 : c0 + 512], start=True, stop=True)
                nc.scalar.copy(out=bias_bc[:, 1024 * h : 1024 * (h + 1)], in_=pb[:])

        def regroup(c):
            blk, g = CHUNKS[c]
            if blk < 2:
                src = w_raw[(blk, g)][:]
            else:
                src = w_raw[(2, g)][:, :, NB * (blk - 2) : NB * (blk - 1)]
            t = wgp.tile([P, NB, 4], BF16, name="wg%d" % c, tag="wg", align_bytes=64)
            wg[c] = t
            cut = NB - P * VSHARE[c]
            if cut > 0:
                nc.scalar.copy(
                    out=t[:, 0:cut, :].rearrange("p (c i) t -> p c t i", i=4),
                    in_=src[:, :, 0:cut].rearrange("p t (c i) -> p c t i", i=4),
                )
            if cut < NB:
                nc.vector.tensor_copy(
                    out=t[:, cut:NB, :].rearrange("p (c i) t -> p c t i", i=4),
                    in_=src[:, :, cut:NB].rearrange("p t (c i) -> p c t i", i=4),
                )

        def quant_w(c):
            nc.vector.quantize_mx(
                out=wc[c][:].bitcast(FP8X4), scales=ws[c][:], in_=wg[c][:].rearrange("p c t -> p (c t)")
            )

        def mx_pass(c, i):
            blk, g = CHUNKS[c]
            if g == 0:
                bank = 4 + i % 4 if blk == 0 else i
                acc[(blk, i)] = ps.tile([P, NB], F32, name="acc%d_%d" % (blk, i), tag="bank%d" % bank)
            nc.tensor.matmul_mx(
                out=acc[(blk, i)][:],
                lhsT=xc[i][:, P * g : P * (g + 1)].bitcast(FP8X4),
                lhsT_scale=xs[i][:, P * g : P * (g + 1)],
                rhs=wc[c][:].bitcast(FP8X4),
                rhs_scale=ws[c][:],
                start=(g == 0),
                stop=(g == PASSES[blk] - 1),
            )

        def evac(blk, i):
            cols = slice(NB * blk, NB * (blk + 1))
            nc.vector.tensor_tensor(out=o_sb[i][:, cols], in0=acc[(blk, i)][:], in1=bias_bc[:, cols], op=ADD)

        def store(i, c0, c1):
            nc.sync.dma_start(out=ov[:, i, c0:c1], in_=o_sb[i][:, c0:c1])

        transposes(0)
        copies(0)
        bias_bcast()
        regroup(0)
        quant_x(0)
        quant_w(0)
        mx_pass(0, 0)
        evac(0, 0)
        for i in range(1, TILES):
            transposes(i)
            copies(i)
            quant_x(i)
            mx_pass(0, i)
            evac(0, i)
        for c in range(1, len(CHUNKS)):
            regroup(c)
            quant_w(c)
        for c in (1, 2):
            for i in range(TILES):
                mx_pass(c, i)
                if c == 2:
                    evac(1, i)
                    store(i, 0, 2 * NB)
        for c in (3, 4, 5, 6):
            for i in range(TILES):
                mx_pass(c, i)
                if c == 6:
                    evac(2, i)
                    store(i, 2 * NB, 3 * NB)
        for i in range(TILES - 1):
            for c in (7, 8, 9, 10):
                mx_pass(c, i)
            evac(3, i)
            store(i, 3 * NB, 4 * NB)
        last = TILES - 1
        for h in range(2):
            half = ps.tile([P, NB // 2], F32, name="half%d" % h, tag="bank%d" % (last if h == 0 else 3))
            cols = slice(NB // 2 * h, NB // 2 * (h + 1))
            for g in range(4):
                nc.tensor.matmul_mx(
                    out=half[:],
                    lhsT=xc[last][:, P * g : P * (g + 1)].bitcast(FP8X4),
                    lhsT_scale=xs[last][:, P * g : P * (g + 1)],
                    rhs=wc[7 + g][:, cols].bitcast(FP8X4),
                    rhs_scale=ws[7 + g][:, cols],
                    start=(g == 0),
                    stop=(g == 3),
                )
            oc = slice(3 * NB + NB // 2 * h, 3 * NB + NB // 2 * (h + 1))
            nc.vector.tensor_tensor(out=o_sb[last][:, oc], in0=half[:], in1=bias_bc[:, oc], op=ADD)
            store(last, 3 * NB + NB // 2 * h, 3 * NB + NB // 2 * (h + 1))
